import numpy as np
import ml_dtypes


def mxq(x, axis, fmt="e4m3"):
    dtype, down = {"e4m3": (ml_dtypes.float8_e4m3fn, 7), "e5m2": (ml_dtypes.float8_e5m2, 14)}[fmt]
    v = np.moveaxis(np.asarray(x, np.float32).astype(ml_dtypes.bfloat16).astype(np.float64), axis, -1)
    blocks = v.reshape(v.shape[:-1] + (-1, 32))
    amax = np.abs(blocks).max(-1, keepdims=True)
    byte = np.maximum(np.where(amax > 0, np.frexp(amax)[1] - 1 + 127, 0) - down, 1)
    scale = np.exp2(byte - 127.0)
    codes = (blocks / scale).astype(np.float32).astype(dtype).astype(np.float64)
    return np.moveaxis((codes * scale).reshape(v.shape), -1, axis)


WIDE = False


def mx_kscale(k):
    if not WIDE:
        return np.ones(k)
    levels = np.array([10, -10, 5, -5, 0])
    a = np.random.permutation(np.resize(levels, k // 512 * 4)).reshape(k // 512, 4)
    idx = np.arange(k)
    return np.exp2(a[idx // 512, idx % 128 // 32])


BF16 = ml_dtypes.bfloat16


def bf(x):
    return np.asarray(x, np.float32).astype(BF16)


def f64(x):
    return np.asarray(x).astype(np.float64)


B, IN, OUT, G = 512, 2048, 2048, 16
CI, CO = IN // G, OUT // G


def setup_inputs():
    s = mx_kscale(IN)
    sg = s.reshape(CI, G)
    return {
        "f_r": bf(np.random.standard_normal((B, CI, G)) * sg),
        "f_i": bf(np.random.standard_normal((B, CI, G)) * sg),
        "log_mag": bf(np.random.standard_normal((B, CI, G)) * 0.7),
        "phase": bf(np.random.uniform(-np.pi, np.pi, (B, CI, G))),
        "r_W": bf(np.random.standard_normal((OUT, IN)) / np.sqrt(IN) / s[None, :]),
        "r_b": bf(np.random.standard_normal(OUT) * 0.3),
        "c_W": bf(np.random.standard_normal((CO, CI)) * 0.5 / np.sqrt(CI)),
        "c_b": bf(np.random.standard_normal(CO) * 0.3),
        "bias_lam": bf(np.random.standard_normal((1, G, CO)) * 0.3),
        "bias_tha": bf(np.random.standard_normal((1, G, CO)) * 0.3),
    }


def reference(f_r, f_i, log_mag, phase, r_W, r_b, c_W, c_b, bias_lam, bias_tha):
    wq = mxq(f64(r_W), 1, "e4m3")
    fr = (mxq(f64(f_r).reshape(B, IN), 1, "e4m3") @ wq.T) + f64(r_b)
    fi = (mxq(f64(f_i).reshape(B, IN), 1, "e4m3") @ wq.T) + f64(r_b)
    fr = fr.reshape(B, CO, G)
    fi = fi.reshape(B, CO, G)
    lT = (f64(log_mag).transpose(0, 2, 1).reshape(B * G, CI) @ f64(c_W).T).reshape(B, G, CO) + f64(c_b) + f64(bias_lam)
    tT = (f64(phase).transpose(0, 2, 1).reshape(B * G, CI) @ f64(c_W).T).reshape(B, G, CO) + f64(c_b) + f64(bias_tha)
    l = np.exp(lT).transpose(0, 2, 1)
    t = tT.transpose(0, 2, 1)
    return fr + l * np.cos(t), fi + l * np.sin(t)

@@ -1,0 +1,292 @@
+import math
+from contextlib import ExitStack
+
+import concourse.mybir as mybir
+from concourse.masks import make_identity
+
+F32 = mybir.dt.float32
+BF16 = mybir.dt.bfloat16
+U32 = mybir.dt.uint32
+U8 = mybir.dt.uint8
+FP8X4 = mybir.dt.float8_e4m3fn_x4
+ALU = mybir.AluOpType
+ACT = mybir.ActivationFunctionType
+
+P = 128
+B, IN, OUT, G = 512, 2048, 2048, 16
+CI, CO = IN // G, OUT // G
+B_TILES = B // P
+BANK = 512
+O_BLOCKS = OUT // BANK
+K_PASS = 4 * P
+PASSES = IN // K_PASS
+G_BANK = BANK // CO
+W_TILES = OUT // P
+AHEAD = 4
+
+TURN = 2.0 * math.pi
+ROUND = 1.5 * 2.0**23
+
+FLOPS = 2 * (2 * B) * IN * OUT + 2 * 2 * (B * G) * CI * CO
+
+
+def tile_bridge_blockv1_pa_kernel(
+    tc, f_r, f_i, log_mag, phase, r_W, r_b, c_W, c_b, bias_lam, bias_tha, out_0, out_1
+):
+    nc = tc.nc
+    with ExitStack() as ctx:
+        const = ctx.enter_context(tc.tile_pool(name="const", bufs=1))
+        raw_pool = ctx.enter_context(tc.tile_pool(name="raw", bufs=AHEAD + 1))
+        flip_pool = ctx.enter_context(tc.tile_pool(name="flip", bufs=2))
+        group_pool = ctx.enter_context(tc.tile_pool(name="group", bufs=3))
+        turn_pool = ctx.enter_context(tc.tile_pool(name="turn", bufs=1))
+        cos_pool = ctx.enter_context(tc.tile_pool(name="cos", bufs=2))
+        stage = ctx.enter_context(tc.tile_pool(name="stage", bufs=4))
+        psum = ctx.enter_context(tc.psum_pool(name="psum", bufs=8))
+
+        def row_tiles(x, n):
+            return [x[i * P : (i + 1) * P, :] for i in range(n)]
+
+        flat = "b c g -> b (c g)"
+        sources = (
+            row_tiles(phase.rearrange(flat), B_TILES)
+            + row_tiles(log_mag.rearrange(flat), B_TILES)
+            + row_tiles(f_r.rearrange(flat), B_TILES)
+            + row_tiles(f_i.rearrange(flat), B_TILES)
+            + row_tiles(r_W, W_TILES)
+        )
+        PHASE0, LOGMAG0, X0, W0 = 0, B_TILES, 2 * B_TILES, 4 * B_TILES
+        raws = []
+
+        def fetch():
+            if len(raws) < len(sources):
+                raw = raw_pool.tile([P, IN], BF16, tag="raw")
+                nc.sync.dma_start(out=raw[:], in_=sources[len(raws)])
+                raws.append(raw)
+
+        ident_f = const.tile([P, P], F32)
+        make_identity(nc, ident_f[:])
+        ident_b = const.tile([P, P], BF16)
+        make_identity(nc, ident_b[:])
+
+        rows = const.tile([P, OUT], BF16)
+        nc.vector.memset(rows[:], 0.0)
+        nc.scalar.dma_start(
+            out=rows[0:1, :].rearrange("o (g c) -> o g c", g=G),
+            in_=c_b.rearrange("(o u c) -> o u c", o=1, u=1).to_broadcast([1, G, CO]),
+        )
+        nc.scalar.dma_start(out=rows[32:33, :], in_=bias_tha.rearrange("o g c -> o (g c)"))
+        nc.scalar.dma_start(out=rows[64:65, :], in_=r_b.rearrange("(o n) -> o n", o=1))
+        nc.scalar.dma_start(out=rows[96:97, :], in_=bias_lam.rearrange("o g c -> o (g c)"))
+        cw_sb = const.tile([P, CI], BF16)
+        nc.scalar.dma_start(out=cw_sb[:], in_=c_W)
+        for unused in range(AHEAD):
+            fetch()
+
+        pick = const.tile([P, 3, P], BF16)
+        PICK_T, PICK_R, PICK_L = 0, 1, 2
+        nc.vector.memset(pick[:], 0.0)
+        nc.vector.memset(pick[0:1, PICK_T, :], 1.0)
+        nc.vector.memset(pick[32:33, PICK_T, :], 1.0)
+        nc.vector.memset(pick[64:65, PICK_R, :], 1.0)
+        nc.vector.memset(pick[0:1, PICK_L, :], 1.0)
+        nc.vector.memset(pick[96:97, PICK_L, :], 1.0)
+
+        cw_bank = psum.tile([P, CO], BF16, tag="bank")
+        nc.tensor.transpose(cw_bank[:], cw_sb[:], ident_b[:])
+        cwT = const.tile([P, CO], BF16)
+        nc.vector.tensor_copy(out=cwT[:], in_=cw_bank[:])
+
+        def bank_by_co(bank):
+            return bank[:].rearrange("p g c -> p c g")
+
+        def tile_by_co(columns, j):
+            return columns.rearrange("p (c g) -> p c g", g=G)[:, :, j * G_BANK : (j + 1) * G_BANK]
+
+        t_bias = const.tile([P, OUT], F32)
+        r_bias = const.tile([P, OUT], F32)
+        for j in range(O_BLOCKS):
+            cols = slice(j * BANK, (j + 1) * BANK)
+            t_bank = psum.tile([P, G_BANK, CO], F32, tag="bank")
+            nc.tensor.matmul(
+                t_bank[:].rearrange("p g c -> p (g c)"),
+                lhsT=pick[:, PICK_T, :], rhs=rows[:, cols], start=True, stop=True,
+            )
+            nc.vector.tensor_scalar(
+                out=tile_by_co(t_bias[:], j), in0=bank_by_co(t_bank),
+                scalar1=1.0 / TURN, scalar2=None, op0=ALU.mult,
+            )
+            r_bank = psum.tile([P, BANK], F32, tag="bank")
+            nc.tensor.matmul(
+                r_bank[:], lhsT=pick[:, PICK_R, :], rhs=rows[:, cols], start=True, stop=True
+            )
+            nc.vector.tensor_copy(out=r_bias[:, cols], in_=r_bank[:])
+
+        def transpose_four(blocks, half):
+            bank = psum.tile([P, 4, P], F32, tag="bank")
+            for q in range(4):
+                nc.tensor.transpose(bank[:, q, :], blocks[:, 4 * half + q, :], ident_f[:])
+            return bank
+
+        def flip_polar(k):
+            fetch()
+            blocks = raws[k][:].bitcast(F32).rearrange("p (c h) -> p h c", h=G // 2)
+            flipped = flip_pool.tile([P, G // 2, P], F32, tag="flipped")
+            for half in range(2):
+                bank = transpose_four(blocks, half)
+                nc.scalar.copy(out=flipped[:, 4 * half : 4 * half + 4, :], in_=bank[:])
+            return flipped[:].rearrange("p h b -> p (h b)").bitcast(BF16).rearrange(
+                "p (h b e) -> p h b e", h=G // 2, e=2
+            )
+
+        def mix_groups(flipped, j, with_bias):
+            bank = psum.tile([P, G_BANK, CO], F32, tag="bank")
+            if with_bias:
+                nc.tensor.matmul(
+                    bank[:].rearrange("p g c -> p (g c)"),
+                    lhsT=pick[:, PICK_L, :], rhs=rows[:, j * BANK : (j + 1) * BANK],
+                    start=True, stop=False,
+                )
+            for gg in range(G_BANK):
+                g = j * G_BANK + gg
+                nc.tensor.matmul(
+                    bank[:, gg, :], lhsT=flipped[:, g // 2, :, g % 2], rhs=cwT[:],
+                    start=not with_bias, stop=(not with_bias) or gg == G_BANK - 1,
+                )
+            return bank
+
+        sin_all = const.tile([P, B_TILES, OUT], F32)
+        exp_all = const.tile([P, B_TILES, OUT], F32)
+
+        def angle_in_turns(bt, flipped):
+            turns = turn_pool.tile([P, OUT], F32, tag="turns")
+            for j in range(O_BLOCKS):
+                bank = mix_groups(flipped, j, False)
+                nc.vector.scalar_tensor_tensor(
+                    out=tile_by_co(turns[:], j), in0=bank_by_co(bank), scalar=1.0 / TURN,
+                    in1=tile_by_co(t_bias[:], j), op0=ALU.mult, op1=ALU.add,
+                )
+            frac = sin_all[:, bt, :]
+            nc.vector.tensor_scalar(
+                out=frac, in0=turns[:], scalar1=ROUND, scalar2=ROUND, op0=ALU.add, op1=ALU.subtract
+            )
+            nc.vector.tensor_tensor(out=frac, in0=turns[:], in1=frac, op=ALU.subtract)
+
+        def magnitude(bt, flipped):
+            for j in range(O_BLOCKS):
+                bank = mix_groups(flipped, j, True)
+                nc.scalar.activation(
+                    out=tile_by_co(exp_all[:, bt, :], j), in_=bank_by_co(bank), func=ACT.Exp
+                )
+
+        def polar_front(first, consume):
+            flipped = flip_polar(first)
+            for bt in range(B_TILES):
+                following = flip_polar(first + bt + 1) if bt + 1 < B_TILES else None
+                consume(bt, flipped)
+                flipped = following
+
+        polar_front(PHASE0, angle_in_turns)
+        polar_front(LOGMAG0, magnitude)
+
+        def polar_back(bt):
+            frac = sin_all[:, bt, :]
+            mag = exp_all[:, bt, :]
+            cos = cos_pool.tile([P, OUT], F32, tag="cos")
+            nc.scalar.activation(out=cos[:], in_=frac, func=ACT.Abs)
+            nc.scalar.activation(out=frac, in_=frac, func=ACT.Sin, scale=TURN)
+            nc.scalar.activation(out=cos[:], in_=cos[:], func=ACT.Sin, scale=-TURN, bias=quarter[:])
+            nc.vector.tensor_tensor(out=frac, in0=frac, in1=mag, op=ALU.mult)
+            nc.vector.tensor_tensor(out=mag, in0=cos[:], in1=mag, op=ALU.mult)
+            nc.vector.tensor_tensor(out=frac, in0=frac, in1=r_bias[:], op=ALU.add)
+            nc.vector.tensor_tensor(out=mag, in0=mag, in1=r_bias[:], op=ALU.add)
+
+        zero = const.tile([P, 1], F32)
+        nc.vector.memset(zero[:], 0.0)
+        quarter = const.tile([P, 1], F32)
+        nc.vector.tensor_scalar(
+            out=quarter[:], in0=zero[:], scalar1=math.pi / 2.0, scalar2=None, op0=ALU.add
+        )
+
+        x_codes = const.tile([P, 2 * B_TILES, PASSES, P], U32, align_bytes=64)
+        x_scales = const.tile([P, 2 * B_TILES, PASSES, P], U8, align_bytes=64)
+        w_codes = const.tile([P, O_BLOCKS, PASSES, BANK], U32, align_bytes=64)
+        w_scales = const.tile([P, O_BLOCKS, PASSES, BANK], U8, align_bytes=64)
+
+        def flip_k(k, half, out_words):
+            blocks = raws[k][:].bitcast(F32).rearrange("p (i w) -> p i w", w=P)
+            bank = transpose_four(blocks, half)
+            nc.scalar.copy(out=out_words, in_=bank[:].rearrange("p (cc u) r -> p cc r u", u=2))
+
+        def quantise(grouped, codes, scales):
+            nc.vector.quantize_mx(out=codes.bitcast(FP8X4), scales=scales, in_=grouped[:])
+
+        def prepare_x(pair):
+            grouped = group_pool.tile([P, 2 * IN], BF16, tag="grouped", align_bytes=64)
+            words = grouped[:].bitcast(F32).rearrange(
+                "p (m c r u) -> p m c r u", m=2, c=PASSES, u=2
+            )
+            for mm in range(2):
+                fetch()
+                for half in range(2):
+                    flip_k(X0 + 2 * pair + mm, half, words[:, mm, 2 * half : 2 * half + 2, :, :])
+            pick_pair = slice(2 * pair, 2 * pair + 2)
+            quantise(
+                grouped,
+                x_codes[:, pick_pair, :, :].rearrange("p m c r -> p (m c r)"),
+                x_scales[:, pick_pair, :, :].rearrange("p m c r -> p (m c r)"),
+            )
+
+        def prepare_w(j):
+            halves = []
+            for half in range(2):
+                grouped = group_pool.tile([P, 2 * IN], BF16, tag="grouped", align_bytes=64)
+                halves.append(grouped)
+            for t in range(BANK // P):
+                fetch()
+                for half in range(2):
+                    words = halves[half][:].bitcast(F32).rearrange(
+                        "p (cc o u) -> p cc o u", cc=2, u=2
+                    )
+                    flip_k(W0 + j * (BANK // P) + t, half, words[:, :, t * P : (t + 1) * P, :])
+            for half in range(2):
+                two = slice(2 * half, 2 * half + 2)
+                quantise(
+                    halves[half],
+                    w_codes[:, j, two, :].rearrange("p c o -> p (c o)"),
+                    w_scales[:, j, two, :].rearrange("p c o -> p (c o)"),
+                )
+
+        def finish(bt):
+            b_rows = slice(bt * P, (bt + 1) * P)
+            for part, polar, out in ((0, exp_all, out_0), (1, sin_all, out_1)):
+                m = part * B_TILES + bt
+                for j in range(O_BLOCKS):
+                    cols = slice(j * BANK, (j + 1) * BANK)
+                    acc = psum.tile([P, BANK], F32, tag="bank")
+                    for c in range(PASSES):
+                        nc.tensor.matmul_mx(
+                            out=acc[:],
+                            lhsT=x_codes[:, m, c, :].bitcast(FP8X4),
+                            lhsT_scale=x_scales[:, m, c, :],
+                            rhs=w_codes[:, j, c, :].bitcast(FP8X4),
+                            rhs_scale=w_scales[:, j, c, :],
+                            start=(c == 0),
+                            stop=(c == PASSES - 1),
+                        )
+                    result = stage.tile([P, BANK], F32, tag="result")
+                    nc.vector.tensor_tensor(
+                        out=result[:], in0=acc[:], in1=polar[:, bt, cols], op=ALU.add
+                    )
+                    nc.sync.dma_start(out=out.rearrange(flat)[b_rows, cols], in_=result[:])
+
+        polar_back(0)
+        for pair in range(B_TILES):
+            prepare_x(pair)
+        polar_back(1)
+        for j in range(O_BLOCKS):
+            prepare_w(j)
+        for bt in range(B_TILES):
+            if bt + 2 < B_TILES:
+                polar_back(bt + 2)
+            finish(bt)

@@ -41,7 +41,7 @@ def tile_bridge_blockv1_pa_kernel(
         group_pool = ctx.enter_context(tc.tile_pool(name="group", bufs=3))
         turn_pool = ctx.enter_context(tc.tile_pool(name="turn", bufs=1))
         cos_pool = ctx.enter_context(tc.tile_pool(name="cos", bufs=2))
-        stage = ctx.enter_context(tc.tile_pool(name="stage", bufs=4))
+        stage = ctx.enter_context(tc.tile_pool(name="stage", bufs=6))
         psum = ctx.enter_context(tc.psum_pool(name="psum", bufs=8))
 
         def row_tiles(x, n):
@@ -198,8 +198,12 @@ def tile_bridge_blockv1_pa_kernel(
             nc.scalar.activation(out=cos[:], in_=cos[:], func=ACT.Sin, scale=-TURN, bias=quarter[:])
             nc.vector.tensor_tensor(out=frac, in0=frac, in1=mag, op=ALU.mult)
             nc.vector.tensor_tensor(out=mag, in0=cos[:], in1=mag, op=ALU.mult)
-            nc.vector.tensor_tensor(out=frac, in0=frac, in1=r_bias[:], op=ALU.add)
-            nc.vector.tensor_tensor(out=mag, in0=mag, in1=r_bias[:], op=ALU.add)
+            for term in (frac, mag):
+                for j in range(O_BLOCKS):
+                    cols = slice(j * BANK, (j + 1) * BANK)
+                    nc.gpsimd.tensor_tensor(
+                        out=term[:, cols], in0=term[:, cols], in1=r_bias[:, cols], op=ALU.add
+                    )
 
         zero = const.tile([P, 1], F32)
         nc.vector.memset(zero[:], 0.0)
@@ -257,36 +261,38 @@ def tile_bridge_blockv1_pa_kernel(
                     w_scales[:, j, two, :].rearrange("p c o -> p (c o)"),
                 )
 
-        def finish(bt):
+        def cell(bt, j):
             b_rows = slice(bt * P, (bt + 1) * P)
+            cols = slice(j * BANK, (j + 1) * BANK)
             for part, polar, out in ((0, exp_all, out_0), (1, sin_all, out_1)):
                 m = part * B_TILES + bt
-                for j in range(O_BLOCKS):
-                    cols = slice(j * BANK, (j + 1) * BANK)
-                    acc = psum.tile([P, BANK], F32, tag="bank")
-                    for c in range(PASSES):
-                        nc.tensor.matmul_mx(
-                            out=acc[:],
-                            lhsT=x_codes[:, m, c, :].bitcast(FP8X4),
-                            lhsT_scale=x_scales[:, m, c, :],
-                            rhs=w_codes[:, j, c, :].bitcast(FP8X4),
-                            rhs_scale=w_scales[:, j, c, :],
-                            start=(c == 0),
-                            stop=(c == PASSES - 1),
-                        )
-                    result = stage.tile([P, BANK], F32, tag="result")
-                    nc.vector.tensor_tensor(
-                        out=result[:], in0=acc[:], in1=polar[:, bt, cols], op=ALU.add
+                acc = psum.tile([P, BANK], F32, tag="bank")
+                for c in range(PASSES):
+                    nc.tensor.matmul_mx(
+                        out=acc[:],
+                        lhsT=x_codes[:, m, c, :].bitcast(FP8X4),
+                        lhsT_scale=x_scales[:, m, c, :],
+                        rhs=w_codes[:, j, c, :].bitcast(FP8X4),
+                        rhs_scale=w_scales[:, j, c, :],
+                        start=(c == 0),
+                        stop=(c == PASSES - 1),
                     )
-                    nc.sync.dma_start(out=out.rearrange(flat)[b_rows, cols], in_=result[:])
+                result = stage.tile([P, BANK], F32, tag="result")
+                nc.vector.tensor_tensor(
+                    out=result[:], in0=acc[:], in1=polar[:, bt, cols], op=ALU.add
+                )
+                nc.sync.dma_start(out=out.rearrange(flat)[b_rows, cols], in_=result[:])
 
         polar_back(0)
         for pair in range(B_TILES):
             prepare_x(pair)
-        polar_back(1)
-        for j in range(O_BLOCKS):
-            prepare_w(j)
-        for bt in range(B_TILES):
-            if bt + 2 < B_TILES:
-                polar_back(bt + 2)
-            finish(bt)
+        prepare_w(0)
+        for s in range(O_BLOCKS):
+            if s + 1 < O_BLOCKS:
+                polar_back(s + 1)
+                prepare_w(s + 1)
+            for bt in range(min(s + 2, B_TILES)):
+                cell(bt, s)
+            if s + 1 < B_TILES:
+                for j in range(s):
+                    cell(s + 1, j)

@@ -43,19 +43,21 @@ def tile_bridge_blockv1_pa_kernel(
         cos_pool = ctx.enter_context(tc.tile_pool(name="cos", bufs=2))
         stage = ctx.enter_context(tc.tile_pool(name="stage", bufs=6))
         psum = ctx.enter_context(tc.psum_pool(name="psum", bufs=8))
+        ctx.enter_context(tc.manual_schedule())
 
         def row_tiles(x, n):
             return [x[i * P : (i + 1) * P, :] for i in range(n)]
 
         flat = "b c g -> b (c g)"
-        sources = (
-            row_tiles(phase.rearrange(flat), B_TILES)
-            + row_tiles(log_mag.rearrange(flat), B_TILES)
-            + row_tiles(f_r.rearrange(flat), B_TILES)
-            + row_tiles(f_i.rearrange(flat), B_TILES)
-            + row_tiles(r_W, W_TILES)
-        )
-        PHASE0, LOGMAG0, X0, W0 = 0, B_TILES, 2 * B_TILES, 4 * B_TILES
+        sources = []
+        for angle_rows, mag_rows in zip(
+            row_tiles(phase.rearrange(flat), B_TILES), row_tiles(log_mag.rearrange(flat), B_TILES)
+        ):
+            sources.extend([angle_rows, mag_rows])
+        sources.extend(row_tiles(f_r.rearrange(flat), B_TILES))
+        sources.extend(row_tiles(f_i.rearrange(flat), B_TILES))
+        sources.extend(row_tiles(r_W, W_TILES))
+        X0, W0 = 2 * B_TILES, 4 * B_TILES
         raws = []
 
         def fetch():
@@ -65,37 +67,50 @@ def tile_bridge_blockv1_pa_kernel(
                 raws.append(raw)
 
         ident_f = const.tile([P, P], F32)
-        make_identity(nc, ident_f[:])
         ident_b = const.tile([P, P], BF16)
-        make_identity(nc, ident_b[:])
-
         rows = const.tile([P, OUT], BF16)
-        nc.vector.memset(rows[:], 0.0)
-        nc.scalar.dma_start(
-            out=rows[0:1, :].rearrange("o (g c) -> o g c", g=G),
-            in_=c_b.rearrange("(o u c) -> o u c", o=1, u=1).to_broadcast([1, G, CO]),
-        )
-        nc.scalar.dma_start(out=rows[32:33, :], in_=bias_tha.rearrange("o g c -> o (g c)"))
-        nc.scalar.dma_start(out=rows[64:65, :], in_=r_b.rearrange("(o n) -> o n", o=1))
-        nc.scalar.dma_start(out=rows[96:97, :], in_=bias_lam.rearrange("o g c -> o (g c)"))
-        cw_sb = const.tile([P, CI], BF16)
-        nc.scalar.dma_start(out=cw_sb[:], in_=c_W)
-        for unused in range(AHEAD):
-            fetch()
-
         pick = const.tile([P, 3, P], BF16)
         PICK_T, PICK_R, PICK_L = 0, 1, 2
-        nc.vector.memset(pick[:], 0.0)
-        nc.vector.memset(pick[0:1, PICK_T, :], 1.0)
-        nc.vector.memset(pick[32:33, PICK_T, :], 1.0)
-        nc.vector.memset(pick[64:65, PICK_R, :], 1.0)
-        nc.vector.memset(pick[0:1, PICK_L, :], 1.0)
-        nc.vector.memset(pick[96:97, PICK_L, :], 1.0)
-
-        cw_bank = psum.tile([P, CO], BF16, tag="bank")
-        nc.tensor.transpose(cw_bank[:], cw_sb[:], ident_b[:])
+        cw_sb = const.tile([P, CI], BF16)
         cwT = const.tile([P, CO], BF16)
-        nc.vector.tensor_copy(out=cwT[:], in_=cw_bank[:])
+        zero = const.tile([P, 1], F32)
+        one = const.tile([P, 1], F32)
+        quarter = const.tile([P, 1], F32)
+        t_bias = const.tile([P, OUT], F32)
+        r_bias = const.tile([P, OUT], F32)
+        sin_all = const.tile([P, B_TILES, OUT], F32)
+        exp_all = const.tile([P, B_TILES, OUT], F32)
+        x_codes = const.tile([P, 2 * B_TILES, PASSES, P], U32, align_bytes=64)
+        x_scales = const.tile([P, 2 * B_TILES, PASSES, P], U8, align_bytes=64)
+        w_codes = const.tile([P, O_BLOCKS, PASSES, BANK], U32, align_bytes=64)
+        w_scales = const.tile([P, O_BLOCKS, PASSES, BANK], U8, align_bytes=64)
+
+        def constants_and_first_loads():
+            nc.vector.memset(rows[:], 0.0)
+            make_identity(nc, ident_f[:])
+            make_identity(nc, ident_b[:])
+            fetch()
+            nc.sync.dma_start(out=cw_sb[:], in_=c_W)
+            nc.sync.dma_start(
+                out=rows[0:1, :].rearrange("o (g c) -> o g c", g=G),
+                in_=c_b.rearrange("(o u c) -> o u c", o=1, u=1).to_broadcast([1, G, CO]),
+            )
+            nc.sync.dma_start(out=rows[32:33, :], in_=bias_tha.rearrange("o g c -> o (g c)"))
+            nc.sync.dma_start(out=rows[96:97, :], in_=bias_lam.rearrange("o g c -> o (g c)"))
+            nc.sync.dma_start(out=rows[64:65, :], in_=r_b.rearrange("(o n) -> o n", o=1))
+            for unused in range(AHEAD - 1):
+                fetch()
+            nc.vector.memset(pick[:], 0.0)
+            nc.vector.memset(pick[0:1, PICK_T, :], 1.0)
+            nc.vector.memset(pick[32:33, PICK_T, :], 1.0)
+            nc.vector.memset(pick[64:65, PICK_R, :], 1.0)
+            nc.vector.memset(pick[0:1, PICK_L, :], 1.0)
+            nc.vector.memset(pick[96:97, PICK_L, :], 1.0)
+            nc.vector.memset(zero[:], 0.0)
+            nc.scalar.activation(out=one[:], in_=zero[:], func=ACT.Exp)
+            nc.vector.tensor_scalar(
+                out=quarter[:], in0=zero[:], scalar1=math.pi / 2.0, scalar2=None, op0=ALU.add
+            )
 
         def bank_by_co(bank):
             return bank[:].rearrange("p g c -> p c g")
@@ -103,24 +118,32 @@ def tile_bridge_blockv1_pa_kernel(
         def tile_by_co(columns, j):
             return columns.rearrange("p (c g) -> p c g", g=G)[:, :, j * G_BANK : (j + 1) * G_BANK]
 
-        t_bias = const.tile([P, OUT], F32)
-        r_bias = const.tile([P, OUT], F32)
-        for j in range(O_BLOCKS):
-            cols = slice(j * BANK, (j + 1) * BANK)
-            t_bank = psum.tile([P, G_BANK, CO], F32, tag="bank")
-            nc.tensor.matmul(
-                t_bank[:].rearrange("p g c -> p (g c)"),
-                lhsT=pick[:, PICK_T, :], rhs=rows[:, cols], start=True, stop=True,
-            )
-            nc.vector.tensor_scalar(
-                out=tile_by_co(t_bias[:], j), in0=bank_by_co(t_bank),
-                scalar1=1.0 / TURN, scalar2=None, op0=ALU.mult,
-            )
-            r_bank = psum.tile([P, BANK], F32, tag="bank")
-            nc.tensor.matmul(
-                r_bank[:], lhsT=pick[:, PICK_R, :], rhs=rows[:, cols], start=True, stop=True
-            )
-            nc.vector.tensor_copy(out=r_bias[:, cols], in_=r_bank[:])
+        def flip_c_w():
+            cw_bank = psum.tile([P, CO], BF16, tag="bank")
+            nc.tensor.transpose(cw_bank[:], cw_sb[:], ident_b[:])
+            nc.vector.tensor_copy(out=cwT[:], in_=cw_bank[:])
+
+        def spread_angle_bias():
+            for j in range(O_BLOCKS):
+                t_bank = psum.tile([P, G_BANK, CO], F32, tag="bank")
+                nc.tensor.matmul(
+                    t_bank[:].rearrange("p g c -> p (g c)"),
+                    lhsT=pick[:, PICK_T, :], rhs=rows[:, j * BANK : (j + 1) * BANK],
+                    start=True, stop=True,
+                )
+                nc.vector.tensor_scalar(
+                    out=tile_by_co(t_bias[:], j), in0=bank_by_co(t_bank),
+                    scalar1=1.0 / TURN, scalar2=None, op0=ALU.mult,
+                )
+
+        def spread_r_b():
+            for j in range(O_BLOCKS):
+                cols = slice(j * BANK, (j + 1) * BANK)
+                r_bank = psum.tile([P, BANK], F32, tag="bank")
+                nc.tensor.matmul(
+                    r_bank[:], lhsT=pick[:, PICK_R, :], rhs=rows[:, cols], start=True, stop=True
+                )
+                nc.vector.tensor_copy(out=r_bias[:, cols], in_=r_bank[:])
 
         def transpose_four(blocks, half):
             bank = psum.tile([P, 4, P], F32, tag="bank")
@@ -155,9 +178,6 @@ def tile_bridge_blockv1_pa_kernel(
                 )
             return bank
 
-        sin_all = const.tile([P, B_TILES, OUT], F32)
-        exp_all = const.tile([P, B_TILES, OUT], F32)
-
         def angle_in_turns(bt, flipped):
             turns = turn_pool.tile([P, OUT], F32, tag="turns")
             for j in range(O_BLOCKS):
@@ -179,16 +199,6 @@ def tile_bridge_blockv1_pa_kernel(
                     out=tile_by_co(exp_all[:, bt, :], j), in_=bank_by_co(bank), func=ACT.Exp
                 )
 
-        def polar_front(first, consume):
-            flipped = flip_polar(first)
-            for bt in range(B_TILES):
-                following = flip_polar(first + bt + 1) if bt + 1 < B_TILES else None
-                consume(bt, flipped)
-                flipped = following
-
-        polar_front(PHASE0, angle_in_turns)
-        polar_front(LOGMAG0, magnitude)
-
         def polar_back(bt):
             frac = sin_all[:, bt, :]
             mag = exp_all[:, bt, :]
@@ -198,24 +208,8 @@ def tile_bridge_blockv1_pa_kernel(
             nc.scalar.activation(out=cos[:], in_=cos[:], func=ACT.Sin, scale=-TURN, bias=quarter[:])
             nc.vector.tensor_tensor(out=frac, in0=frac, in1=mag, op=ALU.mult)
             nc.vector.tensor_tensor(out=mag, in0=cos[:], in1=mag, op=ALU.mult)
-            for term in (frac, mag):
-                for j in range(O_BLOCKS):
-                    cols = slice(j * BANK, (j + 1) * BANK)
-                    nc.gpsimd.tensor_tensor(
-                        out=term[:, cols], in0=term[:, cols], in1=r_bias[:, cols], op=ALU.add
-                    )
-
-        zero = const.tile([P, 1], F32)
-        nc.vector.memset(zero[:], 0.0)
-        quarter = const.tile([P, 1], F32)
-        nc.vector.tensor_scalar(
-            out=quarter[:], in0=zero[:], scalar1=math.pi / 2.0, scalar2=None, op0=ALU.add
-        )
-
-        x_codes = const.tile([P, 2 * B_TILES, PASSES, P], U32, align_bytes=64)
-        x_scales = const.tile([P, 2 * B_TILES, PASSES, P], U8, align_bytes=64)
-        w_codes = const.tile([P, O_BLOCKS, PASSES, BANK], U32, align_bytes=64)
-        w_scales = const.tile([P, O_BLOCKS, PASSES, BANK], U8, align_bytes=64)
+            nc.vector.tensor_tensor(out=frac, in0=frac, in1=r_bias[:], op=ALU.add)
+            nc.vector.tensor_tensor(out=mag, in0=mag, in1=r_bias[:], op=ALU.add)
 
         def flip_k(k, half, out_words):
             blocks = raws[k][:].bitcast(F32).rearrange("p (i w) -> p i w", w=P)
@@ -282,6 +276,20 @@ def tile_bridge_blockv1_pa_kernel(
                     out=result[:], in0=acc[:], in1=polar[:, bt, cols], op=ALU.add
                 )
                 nc.sync.dma_start(out=out.rearrange(flat)[b_rows, cols], in_=result[:])
+
+        constants_and_first_loads()
+        angle_words = flip_polar(0)
+        mag_words = flip_polar(1)
+        flip_c_w()
+        spread_angle_bias()
+        for bt in range(B_TILES):
+            angle_in_turns(bt, angle_words)
+            if bt + 1 < B_TILES:
+                angle_words = flip_polar(2 * bt + 2)
+            magnitude(bt, mag_words)
+            if bt + 1 < B_TILES:
+                mag_words = flip_polar(2 * bt + 3)
+        spread_r_b()
 
         polar_back(0)
         for pair in range(B_TILES):

@@ -49,35 +49,39 @@ def tile_bridge_blockv1_pa_kernel(
             return [x[i * P : (i + 1) * P, :] for i in range(n)]
 
         flat = "b c g -> b (c g)"
+        angle_rows = row_tiles(phase.rearrange(flat), B_TILES)
+        mag_rows = row_tiles(log_mag.rearrange(flat), B_TILES)
+        x_rows = row_tiles(f_r.rearrange(flat), B_TILES) + row_tiles(f_i.rearrange(flat), B_TILES)
         sources = []
-        for angle_rows, mag_rows in zip(
-            row_tiles(phase.rearrange(flat), B_TILES), row_tiles(log_mag.rearrange(flat), B_TILES)
-        ):
-            sources.extend([angle_rows, mag_rows])
-        sources.extend(row_tiles(f_r.rearrange(flat), B_TILES))
-        sources.extend(row_tiles(f_i.rearrange(flat), B_TILES))
-        sources.extend(row_tiles(r_W, W_TILES))
-        X0, W0 = 2 * B_TILES, 4 * B_TILES
-        raws = []
+        for bt in range(B_TILES):
+            angle_source, mag_source = (("angle", bt), angle_rows[bt]), (("mag", bt), mag_rows[bt])
+            if bt < B_TILES - 1:
+                sources.extend([angle_source, mag_source])
+            else:
+                sources.extend([mag_source, angle_source])
+            sources.extend([(("x", 2 * bt + mm), x_rows[2 * bt + mm]) for mm in range(2)])
+        sources.extend([(("w", t), rows_t) for t, rows_t in enumerate(row_tiles(r_W, W_TILES))])
+        raws = {}
 
         def fetch():
             if len(raws) < len(sources):
+                name, rows_of_name = sources[len(raws)]
                 raw = raw_pool.tile([P, IN], BF16, tag="raw")
-                nc.sync.dma_start(out=raw[:], in_=sources[len(raws)])
-                raws.append(raw)
+                nc.sync.dma_start(out=raw[:], in_=rows_of_name)
+                raws[name] = raw
 
         ident_f = const.tile([P, P], F32)
         ident_b = const.tile([P, P], BF16)
         rows = const.tile([P, OUT], BF16)
-        pick = const.tile([P, 3, P], BF16)
-        PICK_T, PICK_R, PICK_L = 0, 1, 2
+        pick = const.tile([P, 2, P], BF16)
+        PICK_T, PICK_L = 0, 1
         cw_sb = const.tile([P, CI], BF16)
         cwT = const.tile([P, CO], BF16)
         zero = const.tile([P, 1], F32)
         one = const.tile([P, 1], F32)
         quarter = const.tile([P, 1], F32)
         t_bias = const.tile([P, OUT], F32)
-        r_bias = const.tile([P, OUT], F32)
+        r_bias = const.tile([P, OUT], BF16)
         sin_all = const.tile([P, B_TILES, OUT], F32)
         exp_all = const.tile([P, B_TILES, OUT], F32)
         x_codes = const.tile([P, 2 * B_TILES, PASSES, P], U32, align_bytes=64)
@@ -97,13 +101,11 @@ def tile_bridge_blockv1_pa_kernel(
             )
             nc.sync.dma_start(out=rows[32:33, :], in_=bias_tha.rearrange("o g c -> o (g c)"))
             nc.sync.dma_start(out=rows[96:97, :], in_=bias_lam.rearrange("o g c -> o (g c)"))
-            nc.sync.dma_start(out=rows[64:65, :], in_=r_b.rearrange("(o n) -> o n", o=1))
             for unused in range(AHEAD - 1):
                 fetch()
             nc.vector.memset(pick[:], 0.0)
             nc.vector.memset(pick[0:1, PICK_T, :], 1.0)
             nc.vector.memset(pick[32:33, PICK_T, :], 1.0)
-            nc.vector.memset(pick[64:65, PICK_R, :], 1.0)
             nc.vector.memset(pick[0:1, PICK_L, :], 1.0)
             nc.vector.memset(pick[96:97, PICK_L, :], 1.0)
             nc.vector.memset(zero[:], 0.0)
@@ -137,13 +139,7 @@ def tile_bridge_blockv1_pa_kernel(
                 )
 
         def spread_r_b():
-            for j in range(O_BLOCKS):
-                cols = slice(j * BANK, (j + 1) * BANK)
-                r_bank = psum.tile([P, BANK], F32, tag="bank")
-                nc.tensor.matmul(
-                    r_bank[:], lhsT=pick[:, PICK_R, :], rhs=rows[:, cols], start=True, stop=True
-                )
-                nc.vector.tensor_copy(out=r_bias[:, cols], in_=r_bank[:])
+            nc.sync.dma_start(out=r_bias[:], in_=r_b.partition_broadcast(P))
 
         def transpose_four(blocks, half):
             bank = psum.tile([P, 4, P], F32, tag="bank")
@@ -151,9 +147,9 @@ def tile_bridge_blockv1_pa_kernel(
                 nc.tensor.transpose(bank[:, q, :], blocks[:, 4 * half + q, :], ident_f[:])
             return bank
 
-        def flip_polar(k):
+        def flip_polar(name):
             fetch()
-            blocks = raws[k][:].bitcast(F32).rearrange("p (c h) -> p h c", h=G // 2)
+            blocks = raws[name][:].bitcast(F32).rearrange("p (c h) -> p h c", h=G // 2)
             flipped = flip_pool.tile([P, G // 2, P], F32, tag="flipped")
             for half in range(2):
                 bank = transpose_four(blocks, half)
@@ -199,27 +195,31 @@ def tile_bridge_blockv1_pa_kernel(
                     out=tile_by_co(exp_all[:, bt, :], j), in_=bank_by_co(bank), func=ACT.Exp
                 )
 
-        def polar_back(bt):
+        def sine_and_cosine(bt):
             frac = sin_all[:, bt, :]
-            mag = exp_all[:, bt, :]
             cos = cos_pool.tile([P, OUT], F32, tag="cos")
             nc.scalar.activation(out=cos[:], in_=frac, func=ACT.Abs)
             nc.scalar.activation(out=frac, in_=frac, func=ACT.Sin, scale=TURN)
             nc.scalar.activation(out=cos[:], in_=cos[:], func=ACT.Sin, scale=-TURN, bias=quarter[:])
+            return cos
+
+        def polar_terms(bt, cos):
+            frac = sin_all[:, bt, :]
+            mag = exp_all[:, bt, :]
             nc.vector.tensor_tensor(out=frac, in0=frac, in1=mag, op=ALU.mult)
             nc.vector.tensor_tensor(out=mag, in0=cos[:], in1=mag, op=ALU.mult)
             nc.vector.tensor_tensor(out=frac, in0=frac, in1=r_bias[:], op=ALU.add)
             nc.vector.tensor_tensor(out=mag, in0=mag, in1=r_bias[:], op=ALU.add)
 
-        def flip_k(k, half, out_words):
-            blocks = raws[k][:].bitcast(F32).rearrange("p (i w) -> p i w", w=P)
+        def flip_k(name, half, out_words):
+            blocks = raws[name][:].bitcast(F32).rearrange("p (i w) -> p i w", w=P)
             bank = transpose_four(blocks, half)
             nc.scalar.copy(out=out_words, in_=bank[:].rearrange("p (cc u) r -> p cc r u", u=2))
 
         def quantise(grouped, codes, scales):
             nc.vector.quantize_mx(out=codes.bitcast(FP8X4), scales=scales, in_=grouped[:])
 
-        def prepare_x(pair):
+        def flip_x(pair):
             grouped = group_pool.tile([P, 2 * IN], BF16, tag="grouped", align_bytes=64)
             words = grouped[:].bitcast(F32).rearrange(
                 "p (m c r u) -> p m c r u", m=2, c=PASSES, u=2
@@ -227,7 +227,10 @@ def tile_bridge_blockv1_pa_kernel(
             for mm in range(2):
                 fetch()
                 for half in range(2):
-                    flip_k(X0 + 2 * pair + mm, half, words[:, mm, 2 * half : 2 * half + 2, :, :])
+                    flip_k(("x", 2 * pair + mm), half, words[:, mm, 2 * half : 2 * half + 2, :, :])
+            return grouped
+
+        def quantise_x(pair, grouped):
             pick_pair = slice(2 * pair, 2 * pair + 2)
             quantise(
                 grouped,
@@ -246,7 +249,7 @@ def tile_bridge_blockv1_pa_kernel(
                     words = halves[half][:].bitcast(F32).rearrange(
                         "p (cc o u) -> p cc o u", cc=2, u=2
                     )
-                    flip_k(W0 + j * (BANK // P) + t, half, words[:, :, t * P : (t + 1) * P, :])
+                    flip_k(("w", j * (BANK // P) + t), half, words[:, :, t * P : (t + 1) * P, :])
             for half in range(2):
                 two = slice(2 * half, 2 * half + 2)
                 quantise(
@@ -278,26 +281,37 @@ def tile_bridge_blockv1_pa_kernel(
                 nc.sync.dma_start(out=out.rearrange(flat)[b_rows, cols], in_=result[:])
 
         constants_and_first_loads()
-        angle_words = flip_polar(0)
-        mag_words = flip_polar(1)
+        words_of = {("angle", 0): flip_polar(("angle", 0)), ("mag", 0): flip_polar(("mag", 0))}
         flip_c_w()
         spread_angle_bias()
+        LAST = B_TILES - 1
+        x_grouped = {}
+        cos_of = {}
         for bt in range(B_TILES):
-            angle_in_turns(bt, angle_words)
-            if bt + 1 < B_TILES:
-                angle_words = flip_polar(2 * bt + 2)
-            magnitude(bt, mag_words)
-            if bt + 1 < B_TILES:
-                mag_words = flip_polar(2 * bt + 3)
-        spread_r_b()
+            if bt < LAST:
+                x_grouped[bt] = flip_x(bt)
+            else:
+                cos_of[0] = sine_and_cosine(0)
+            angle_in_turns(bt, words_of[("angle", bt)])
+            if bt > 0 and bt < LAST:
+                quantise_x(bt - 1, x_grouped[bt - 1])
+            if bt < LAST:
+                first, second = ("angle", "mag") if bt + 1 < LAST else ("mag", "angle")
+                words_of[(first, bt + 1)] = flip_polar((first, bt + 1))
+                magnitude(bt, words_of[("mag", bt)])
+                words_of[(second, bt + 1)] = flip_polar((second, bt + 1))
+            if bt == 1:
+                spread_r_b()
+            if bt + 1 == LAST:
+                quantise_x(bt, x_grouped[bt])
+                magnitude(LAST, words_of[("mag", LAST)])
 
-        polar_back(0)
-        for pair in range(B_TILES):
-            prepare_x(pair)
+        polar_terms(0, cos_of[0])
+        quantise_x(LAST, flip_x(LAST))
         prepare_w(0)
         for s in range(O_BLOCKS):
             if s + 1 < O_BLOCKS:
-                polar_back(s + 1)
+                polar_terms(s + 1, sine_and_cosine(s + 1))
                 prepare_w(s + 1)
             for bt in range(min(s + 2, B_TILES)):
                 cell(bt, s)

@@ -203,13 +203,29 @@ def tile_bridge_blockv1_pa_kernel(
             nc.scalar.activation(out=cos[:], in_=cos[:], func=ACT.Sin, scale=-TURN, bias=quarter[:])
             return cos
 
-        def polar_terms(bt, cos):
+        def polar_products(bt, cos):
             frac = sin_all[:, bt, :]
             mag = exp_all[:, bt, :]
             nc.vector.tensor_tensor(out=frac, in0=frac, in1=mag, op=ALU.mult)
             nc.vector.tensor_tensor(out=mag, in0=cos[:], in1=mag, op=ALU.mult)
+
+        def add_r_b(bt):
+            frac = sin_all[:, bt, :]
+            mag = exp_all[:, bt, :]
             nc.vector.tensor_tensor(out=frac, in0=frac, in1=r_bias[:], op=ALU.add)
             nc.vector.tensor_tensor(out=mag, in0=mag, in1=r_bias[:], op=ALU.add)
+
+        def add_r_b_on_gpsimd(bt):
+            for j in range(O_BLOCKS):
+                cols = slice(j * BANK, (j + 1) * BANK)
+                for polar in (exp_all, sin_all):
+                    nc.gpsimd.tensor_tensor(
+                        out=polar[:, bt, cols], in0=polar[:, bt, cols], in1=r_bias[:, cols], op=ALU.add
+                    )
+
+        def polar_terms(bt, cos):
+            polar_products(bt, cos)
+            add_r_b(bt)
 
         def flip_k(name, half, out_words):
             blocks = raws[name][:].bitcast(F32).rearrange("p (i w) -> p i w", w=P)
@@ -310,11 +326,17 @@ def tile_bridge_blockv1_pa_kernel(
         quantise_x(LAST, flip_x(LAST))
         prepare_w(0)
         for s in range(O_BLOCKS):
-            if s + 1 < O_BLOCKS:
+            if s + 1 < LAST:
                 polar_terms(s + 1, sine_and_cosine(s + 1))
                 prepare_w(s + 1)
-            for bt in range(min(s + 2, B_TILES)):
+            if s + 1 == LAST:
+                polar_products(LAST, sine_and_cosine(LAST))
+                prepare_w(LAST)
+                add_r_b_on_gpsimd(LAST)
+            for bt in range(min(s + 2, LAST)):
                 cell(bt, s)
-            if s + 1 < B_TILES:
+            if s + 1 < LAST:
                 for j in range(s):
                     cell(s + 1, j)
+        for j in range(O_BLOCKS):
+            cell(LAST, j)

@@ -182,11 +182,20 @@ def tile_bridge_blockv1_pa_kernel(
                     out=tile_by_co(turns[:], j), in0=bank_by_co(bank), scalar=1.0 / TURN,
                     in1=tile_by_co(t_bias[:], j), op0=ALU.mult, op1=ALU.add,
                 )
-            frac = sin_all[:, bt, :]
-            nc.vector.tensor_scalar(
-                out=frac, in0=turns[:], scalar1=ROUND, scalar2=ROUND, op0=ALU.add, op1=ALU.subtract
-            )
-            nc.vector.tensor_tensor(out=frac, in0=turns[:], in1=frac, op=ALU.subtract)
+            return turns
+
+        def fraction_of_turn(bt, turns):
+            halves = (slice(0, OUT // 2), slice(OUT // 2, OUT))
+            for cols in halves:
+                nc.vector.tensor_scalar(
+                    out=sin_all[:, bt, cols], in0=turns[:, cols], scalar1=ROUND, scalar2=ROUND,
+                    op0=ALU.add, op1=ALU.subtract,
+                )
+            for cols in halves:
+                nc.vector.tensor_tensor(
+                    out=sin_all[:, bt, cols], in0=turns[:, cols], in1=sin_all[:, bt, cols],
+                    op=ALU.subtract,
+                )
 
         def magnitude(bt, flipped):
             for j in range(O_BLOCKS):
@@ -297,9 +306,10 @@ def tile_bridge_blockv1_pa_kernel(
                 nc.sync.dma_start(out=out.rearrange(flat)[b_rows, cols], in_=result[:])
 
         constants_and_first_loads()
-        words_of = {("angle", 0): flip_polar(("angle", 0)), ("mag", 0): flip_polar(("mag", 0))}
+        words_of = {("angle", 0): flip_polar(("angle", 0))}
         flip_c_w()
         spread_angle_bias()
+        words_of[("mag", 0)] = flip_polar(("mag", 0))
         LAST = B_TILES - 1
         x_grouped = {}
         cos_of = {}
@@ -308,9 +318,10 @@ def tile_bridge_blockv1_pa_kernel(
                 x_grouped[bt] = flip_x(bt)
             else:
                 cos_of[0] = sine_and_cosine(0)
-            angle_in_turns(bt, words_of[("angle", bt)])
-            if bt > 0 and bt < LAST:
+            turns = angle_in_turns(bt, words_of[("angle", bt)])
+            if bt > 0:
                 quantise_x(bt - 1, x_grouped[bt - 1])
+            fraction_of_turn(bt, turns)
             if bt < LAST:
                 first, second = ("angle", "mag") if bt + 1 < LAST else ("mag", "angle")
                 words_of[(first, bt + 1)] = flip_polar((first, bt + 1))
@@ -319,7 +330,6 @@ def tile_bridge_blockv1_pa_kernel(
             if bt == 1:
                 spread_r_b()
             if bt + 1 == LAST:
-                quantise_x(bt, x_grouped[bt])
                 magnitude(LAST, words_of[("mag", LAST)])
 
         polar_terms(0, cos_of[0])

@@ -340,8 +340,9 @@ def tile_bridge_blockv1_pa_kernel(
                 polar_terms(s + 1, sine_and_cosine(s + 1))
                 prepare_w(s + 1)
             if s + 1 == LAST:
-                polar_products(LAST, sine_and_cosine(LAST))
+                cos_of[LAST] = sine_and_cosine(LAST)
                 prepare_w(LAST)
+                polar_products(LAST, cos_of[LAST])
                 add_r_b_on_gpsimd(LAST)
             for bt in range(min(s + 2, LAST)):
                 cell(bt, s)

@@ -79,7 +79,6 @@ def tile_bridge_blockv1_pa_kernel(
         cwT = const.tile([P, CO], BF16)
         zero = const.tile([P, 1], F32)
         one = const.tile([P, 1], F32)
-        quarter = const.tile([P, 1], F32)
         t_bias = const.tile([P, OUT], F32)
         r_bias = const.tile([P, OUT], BF16)
         sin_all = const.tile([P, B_TILES, OUT], F32)
@@ -110,9 +109,6 @@ def tile_bridge_blockv1_pa_kernel(
             nc.vector.memset(pick[96:97, PICK_L, :], 1.0)
             nc.vector.memset(zero[:], 0.0)
             nc.scalar.activation(out=one[:], in_=zero[:], func=ACT.Exp)
-            nc.vector.tensor_scalar(
-                out=quarter[:], in0=zero[:], scalar1=math.pi / 2.0, scalar2=None, op0=ALU.add
-            )
 
         def bank_by_co(bank):
             return bank[:].rearrange("p g c -> p c g")
@@ -209,7 +205,7 @@ def tile_bridge_blockv1_pa_kernel(
             cos = cos_pool.tile([P, OUT], F32, tag="cos")
             nc.scalar.activation(out=cos[:], in_=frac, func=ACT.Abs)
             nc.scalar.activation(out=frac, in_=frac, func=ACT.Sin, scale=TURN)
-            nc.scalar.activation(out=cos[:], in_=cos[:], func=ACT.Sin, scale=-TURN, bias=quarter[:])
+            nc.scalar.activation(out=cos[:], in_=cos[:], func=ACT.Sin, scale=-TURN, bias=math.pi / 2.0)
             return cos
 
         def polar_products(bt, cos):
@@ -336,8 +332,12 @@ def tile_bridge_blockv1_pa_kernel(
         quantise_x(LAST, flip_x(LAST))
         prepare_w(0)
         for s in range(O_BLOCKS):
-            if s + 1 < LAST:
+            if s + 1 < LAST - 1:
                 polar_terms(s + 1, sine_and_cosine(s + 1))
+                prepare_w(s + 1)
+            if s + 1 == LAST - 1:
+                polar_products(s + 1, sine_and_cosine(s + 1))
+                add_r_b_on_gpsimd(s + 1)
                 prepare_w(s + 1)
             if s + 1 == LAST:
                 cos_of[LAST] = sine_and_cosine(LAST)

import math
from contextlib import ExitStack

import concourse.mybir as mybir
from concourse.masks import make_identity

F32 = mybir.dt.float32
BF16 = mybir.dt.bfloat16
U32 = mybir.dt.uint32
U8 = mybir.dt.uint8
FP8X4 = mybir.dt.float8_e4m3fn_x4
ALU = mybir.AluOpType
ACT = mybir.ActivationFunctionType

P = 128
B, IN, OUT, G = 512, 2048, 2048, 16
CI, CO = IN // G, OUT // G
B_TILES = B // P
BANK = 512
O_BLOCKS = OUT // BANK
K_PASS = 4 * P
PASSES = IN // K_PASS
G_BANK = BANK // CO
W_TILES = OUT // P
AHEAD = 4

TURN = 2.0 * math.pi
ROUND = 1.5 * 2.0**23

FLOPS = 2 * (2 * B) * IN * OUT + 2 * 2 * (B * G) * CI * CO


def tile_bridge_blockv1_pa_kernel(
    tc, f_r, f_i, log_mag, phase, r_W, r_b, c_W, c_b, bias_lam, bias_tha, out_0, out_1
):
    nc = tc.nc
    with ExitStack() as ctx:
        const = ctx.enter_context(tc.tile_pool(name="const", bufs=1))
        raw_pool = ctx.enter_context(tc.tile_pool(name="raw", bufs=AHEAD + 1))
        flip_pool = ctx.enter_context(tc.tile_pool(name="flip", bufs=2))
        group_pool = ctx.enter_context(tc.tile_pool(name="group", bufs=3))
        turn_pool = ctx.enter_context(tc.tile_pool(name="turn", bufs=1))
        cos_pool = ctx.enter_context(tc.tile_pool(name="cos", bufs=2))
        stage = ctx.enter_context(tc.tile_pool(name="stage", bufs=6))
        psum = ctx.enter_context(tc.psum_pool(name="psum", bufs=8))
        ctx.enter_context(tc.manual_schedule())

        def row_tiles(x, n):
            return [x[i * P : (i + 1) * P, :] for i in range(n)]

        flat = "b c g -> b (c g)"
        angle_rows = row_tiles(phase.rearrange(flat), B_TILES)
        mag_rows = row_tiles(log_mag.rearrange(flat), B_TILES)
        x_rows = row_tiles(f_r.rearrange(flat), B_TILES) + row_tiles(f_i.rearrange(flat), B_TILES)
        sources = []
        for bt in range(B_TILES):
            angle_source, mag_source = (("angle", bt), angle_rows[bt]), (("mag", bt), mag_rows[bt])
            if bt < B_TILES - 1:
                sources.extend([angle_source, mag_source])
            else:
                sources.extend([mag_source, angle_source])
            sources.extend([(("x", 2 * bt + mm), x_rows[2 * bt + mm]) for mm in range(2)])
        sources.extend([(("w", t), rows_t) for t, rows_t in enumerate(row_tiles(r_W, W_TILES))])
        raws = {}

        def fetch():
            if len(raws) < len(sources):
                name, rows_of_name = sources[len(raws)]
                raw = raw_pool.tile([P, IN], BF16, tag="raw")
                nc.sync.dma_start(out=raw[:], in_=rows_of_name)
                raws[name] = raw

        ident_f = const.tile([P, P], F32)
        ident_b = const.tile([P, P], BF16)
        rows = const.tile([P, OUT], BF16)
        pick = const.tile([P, 2, P], BF16)
        PICK_T, PICK_L = 0, 1
        cw_sb = const.tile([P, CI], BF16)
        cwT = const.tile([P, CO], BF16)
        zero = const.tile([P, 1], F32)
        one = const.tile([P, 1], F32)
        t_bias = const.tile([P, OUT], F32)
        r_bias = const.tile([P, OUT], BF16)
        sin_all = const.tile([P, B_TILES, OUT], F32)
        exp_all = const.tile([P, B_TILES, OUT], F32)
        x_codes = const.tile([P, 2 * B_TILES, PASSES, P], U32, align_bytes=64)
        x_scales = const.tile([P, 2 * B_TILES, PASSES, P], U8, align_bytes=64)
        w_codes = const.tile([P, O_BLOCKS, PASSES, BANK], U32, align_bytes=64)
        w_scales = const.tile([P, O_BLOCKS, PASSES, BANK], U8, align_bytes=64)

        def constants_and_first_loads():
            nc.vector.memset(rows[:], 0.0)
            make_identity(nc, ident_f[:])
            make_identity(nc, ident_b[:])
            fetch()
            nc.sync.dma_start(out=cw_sb[:], in_=c_W)
            nc.sync.dma_start(
                out=rows[0:1, :].rearrange("o (g c) -> o g c", g=G),
                in_=c_b.rearrange("(o u c) -> o u c", o=1, u=1).to_broadcast([1, G, CO]),
            )
            nc.sync.dma_start(out=rows[32:33, :], in_=bias_tha.rearrange("o g c -> o (g c)"))
            nc.sync.dma_start(out=rows[96:97, :], in_=bias_lam.rearrange("o g c -> o (g c)"))
            for unused in range(AHEAD - 1):
                fetch()
            nc.vector.memset(pick[:], 0.0)
            nc.vector.memset(pick[0:1, PICK_T, :], 1.0)
            nc.vector.memset(pick[32:33, PICK_T, :], 1.0)
            nc.vector.memset(pick[0:1, PICK_L, :], 1.0)
            nc.vector.memset(pick[96:97, PICK_L, :], 1.0)
            nc.vector.memset(zero[:], 0.0)
            nc.scalar.activation(out=one[:], in_=zero[:], func=ACT.Exp)

        def bank_by_co(bank):
            return bank[:].rearrange("p g c -> p c g")

        def tile_by_co(columns, j):
            return columns.rearrange("p (c g) -> p c g", g=G)[:, :, j * G_BANK : (j + 1) * G_BANK]

        def flip_c_w():
            cw_bank = psum.tile([P, CO], BF16, tag="bank")
            nc.tensor.transpose(cw_bank[:], cw_sb[:], ident_b[:])
            nc.vector.tensor_copy(out=cwT[:], in_=cw_bank[:])

        def spread_angle_bias():
            for j in range(O_BLOCKS):
                t_bank = psum.tile([P, G_BANK, CO], F32, tag="bank")
                nc.tensor.matmul(
                    t_bank[:].rearrange("p g c -> p (g c)"),
                    lhsT=pick[:, PICK_T, :], rhs=rows[:, j * BANK : (j + 1) * BANK],
                    start=True, stop=True,
                )
                nc.vector.tensor_scalar(
                    out=tile_by_co(t_bias[:], j), in0=bank_by_co(t_bank),
                    scalar1=1.0 / TURN, scalar2=None, op0=ALU.mult,
                )

        def spread_r_b():
            nc.sync.dma_start(out=r_bias[:], in_=r_b.partition_broadcast(P))

        def transpose_four(blocks, half):
            bank = psum.tile([P, 4, P], F32, tag="bank")
            for q in range(4):
                nc.tensor.transpose(bank[:, q, :], blocks[:, 4 * half + q, :], ident_f[:])
            return bank

        def flip_polar(name):
            fetch()
            blocks = raws[name][:].bitcast(F32).rearrange("p (c h) -> p h c", h=G // 2)
            flipped = flip_pool.tile([P, G // 2, P], F32, tag="flipped")
            for half in range(2):
                bank = transpose_four(blocks, half)
                nc.scalar.copy(out=flipped[:, 4 * half : 4 * half + 4, :], in_=bank[:])
            return flipped[:].rearrange("p h b -> p (h b)").bitcast(BF16).rearrange(
                "p (h b e) -> p h b e", h=G // 2, e=2
            )

        def mix_groups(flipped, j, with_bias):
            bank = psum.tile([P, G_BANK, CO], F32, tag="bank")
            if with_bias:
                nc.tensor.matmul(
                    bank[:].rearrange("p g c -> p (g c)"),
                    lhsT=pick[:, PICK_L, :], rhs=rows[:, j * BANK : (j + 1) * BANK],
                    start=True, stop=False,
                )
            for gg in range(G_BANK):
                g = j * G_BANK + gg
                nc.tensor.matmul(
                    bank[:, gg, :], lhsT=flipped[:, g // 2, :, g % 2], rhs=cwT[:],
                    start=not with_bias, stop=(not with_bias) or gg == G_BANK - 1,
                )
            return bank

        def angle_in_turns(bt, flipped):
            turns = turn_pool.tile([P, OUT], F32, tag="turns")
            for j in range(O_BLOCKS):
                bank = mix_groups(flipped, j, False)
                nc.vector.scalar_tensor_tensor(
                    out=tile_by_co(turns[:], j), in0=bank_by_co(bank), scalar=1.0 / TURN,
                    in1=tile_by_co(t_bias[:], j), op0=ALU.mult, op1=ALU.add,
                )
            return turns

        def fraction_of_turn(bt, turns):
            halves = (slice(0, OUT // 2), slice(OUT // 2, OUT))
            for cols in halves:
                nc.vector.tensor_scalar(
                    out=sin_all[:, bt, cols], in0=turns[:, cols], scalar1=ROUND, scalar2=ROUND,
                    op0=ALU.add, op1=ALU.subtract,
                )
            for cols in halves:
                nc.vector.tensor_tensor(
                    out=sin_all[:, bt, cols], in0=turns[:, cols], in1=sin_all[:, bt, cols],
                    op=ALU.subtract,
                )

        def magnitude(bt, flipped):
            for j in range(O_BLOCKS):
                bank = mix_groups(flipped, j, True)
                nc.scalar.activation(
                    out=tile_by_co(exp_all[:, bt, :], j), in_=bank_by_co(bank), func=ACT.Exp
                )

        def sine_and_cosine(bt):
            frac = sin_all[:, bt, :]
            cos = cos_pool.tile([P, OUT], F32, tag="cos")
            nc.scalar.activation(out=cos[:], in_=frac, func=ACT.Abs)
            nc.scalar.activation(out=frac, in_=frac, func=ACT.Sin, scale=TURN)
            nc.scalar.activation(out=cos[:], in_=cos[:], func=ACT.Sin, scale=-TURN, bias=math.pi / 2.0)
            return cos

        def polar_products(bt, cos):
            frac = sin_all[:, bt, :]
            mag = exp_all[:, bt, :]
            nc.vector.tensor_tensor(out=frac, in0=frac, in1=mag, op=ALU.mult)
            nc.vector.tensor_tensor(out=mag, in0=cos[:], in1=mag, op=ALU.mult)

        def add_r_b(bt):
            frac = sin_all[:, bt, :]
            mag = exp_all[:, bt, :]
            nc.vector.tensor_tensor(out=frac, in0=frac, in1=r_bias[:], op=ALU.add)
            nc.vector.tensor_tensor(out=mag, in0=mag, in1=r_bias[:], op=ALU.add)

        def add_r_b_on_gpsimd(bt):
            for j in range(O_BLOCKS):
                cols = slice(j * BANK, (j + 1) * BANK)
                for polar in (exp_all, sin_all):
                    nc.gpsimd.tensor_tensor(
                        out=polar[:, bt, cols], in0=polar[:, bt, cols], in1=r_bias[:, cols], op=ALU.add
                    )

        def polar_terms(bt, cos):
            polar_products(bt, cos)
            add_r_b(bt)

        def flip_k(name, half, out_words):
            blocks = raws[name][:].bitcast(F32).rearrange("p (i w) -> p i w", w=P)
            bank = transpose_four(blocks, half)
            nc.scalar.copy(out=out_words, in_=bank[:].rearrange("p (cc u) r -> p cc r u", u=2))

        def quantise(grouped, codes, scales):
            nc.vector.quantize_mx(out=codes.bitcast(FP8X4), scales=scales, in_=grouped[:])

        def flip_x(pair):
            grouped = group_pool.tile([P, 2 * IN], BF16, tag="grouped", align_bytes=64)
            words = grouped[:].bitcast(F32).rearrange(
                "p (m c r u) -> p m c r u", m=2, c=PASSES, u=2
            )
            for mm in range(2):
                fetch()
                for half in range(2):
                    flip_k(("x", 2 * pair + mm), half, words[:, mm, 2 * half : 2 * half + 2, :, :])
            return grouped

        def quantise_x(pair, grouped):
            pick_pair = slice(2 * pair, 2 * pair + 2)
            quantise(
                grouped,
                x_codes[:, pick_pair, :, :].rearrange("p m c r -> p (m c r)"),
                x_scales[:, pick_pair, :, :].rearrange("p m c r -> p (m c r)"),
            )

        def prepare_w(j):
            halves = []
            for half in range(2):
                grouped = group_pool.tile([P, 2 * IN], BF16, tag="grouped", align_bytes=64)
                halves.append(grouped)
            for t in range(BANK // P):
                fetch()
                for half in range(2):
                    words = halves[half][:].bitcast(F32).rearrange(
                        "p (cc o u) -> p cc o u", cc=2, u=2
                    )
                    flip_k(("w", j * (BANK // P) + t), half, words[:, :, t * P : (t + 1) * P, :])
            for half in range(2):
                two = slice(2 * half, 2 * half + 2)
                quantise(
                    halves[half],
                    w_codes[:, j, two, :].rearrange("p c o -> p (c o)"),
                    w_scales[:, j, two, :].rearrange("p c o -> p (c o)"),
                )

        def cell(bt, j):
            b_rows = slice(bt * P, (bt + 1) * P)
            cols = slice(j * BANK, (j + 1) * BANK)
            for part, polar, out in ((0, exp_all, out_0), (1, sin_all, out_1)):
                m = part * B_TILES + bt
                acc = psum.tile([P, BANK], F32, tag="bank")
                for c in range(PASSES):
                    nc.tensor.matmul_mx(
                        out=acc[:],
                        lhsT=x_codes[:, m, c, :].bitcast(FP8X4),
                        lhsT_scale=x_scales[:, m, c, :],
                        rhs=w_codes[:, j, c, :].bitcast(FP8X4),
                        rhs_scale=w_scales[:, j, c, :],
                        start=(c == 0),
                        stop=(c == PASSES - 1),
                    )
                result = stage.tile([P, BANK], F32, tag="result")
                nc.vector.tensor_tensor(
                    out=result[:], in0=acc[:], in1=polar[:, bt, cols], op=ALU.add
                )
                nc.sync.dma_start(out=out.rearrange(flat)[b_rows, cols], in_=result[:])

        constants_and_first_loads()
        words_of = {("angle", 0): flip_polar(("angle", 0))}
        flip_c_w()
        spread_angle_bias()
        words_of[("mag", 0)] = flip_polar(("mag", 0))
        LAST = B_TILES - 1
        x_grouped = {}
        cos_of = {}
        for bt in range(B_TILES):
            if bt < LAST:
                x_grouped[bt] = flip_x(bt)
            else:
                cos_of[0] = sine_and_cosine(0)
            turns = angle_in_turns(bt, words_of[("angle", bt)])
            if bt > 0:
                quantise_x(bt - 1, x_grouped[bt - 1])
            fraction_of_turn(bt, turns)
            if bt < LAST:
                first, second = ("angle", "mag") if bt + 1 < LAST else ("mag", "angle")
                words_of[(first, bt + 1)] = flip_polar((first, bt + 1))
                magnitude(bt, words_of[("mag", bt)])
                words_of[(second, bt + 1)] = flip_polar((second, bt + 1))
            if bt == 1:
                spread_r_b()
            if bt + 1 == LAST:
                magnitude(LAST, words_of[("mag", LAST)])

        polar_terms(0, cos_of[0])
        quantise_x(LAST, flip_x(LAST))
        prepare_w(0)
        for s in range(O_BLOCKS):
            if s + 1 < LAST - 1:
                polar_terms(s + 1, sine_and_cosine(s + 1))
                prepare_w(s + 1)
            if s + 1 == LAST - 1:
                polar_products(s + 1, sine_and_cosine(s + 1))
                add_r_b_on_gpsimd(s + 1)
                prepare_w(s + 1)
            if s + 1 == LAST:
                cos_of[LAST] = sine_and_cosine(LAST)
                prepare_w(LAST)
                polar_products(LAST, cos_of[LAST])
                add_r_b_on_gpsimd(LAST)
            for bt in range(min(s + 2, LAST)):
                cell(bt, s)
            if s + 1 < LAST:
                for j in range(s):
                    cell(s + 1, j)
        for j in range(O_BLOCKS):
            cell(LAST, j)
